import numpy as np
import ml_dtypes


def mxq(x, axis, fmt="e4m3"):
    dtype, down = {"e4m3": (ml_dtypes.float8_e4m3fn, 7), "e5m2": (ml_dtypes.float8_e5m2, 14)}[fmt]
    v = np.moveaxis(np.asarray(x, np.float32).astype(ml_dtypes.bfloat16).astype(np.float64), axis, -1)
    blocks = v.reshape(v.shape[:-1] + (-1, 32))
    amax = np.abs(blocks).max(-1, keepdims=True)
    byte = np.maximum(np.where(amax > 0, np.frexp(amax)[1] - 1 + 127, 0) - down, 1)
    scale = np.exp2(byte - 127.0)
    codes = (blocks / scale).astype(np.float32).astype(dtype).astype(np.float64)
    return np.moveaxis((codes * scale).reshape(v.shape), -1, axis)


WIDE = False


def mx_kscale(k):
    if not WIDE:
        return np.ones(k)
    levels = np.array([10, -10, 5, -5, 0])
    a = np.random.permutation(np.resize(levels, k // 512 * 4)).reshape(k // 512, 4)
    idx = np.arange(k)
    return np.exp2(a[idx // 512, idx % 128 // 32])


BF16 = ml_dtypes.bfloat16


def bf(x):
    return np.asarray(x, np.float32).astype(BF16)


def f64(x):
    return np.asarray(x).astype(np.float64)


N, P, D, E, F = 1024, 3, 512, 1024, 1024
BN_EPS = 1e-5


def setup_inputs():
    t = mx_kscale(E)
    h = 1.2 * np.random.standard_normal((N, P, E)) + 0.6 * np.random.standard_normal((1, P, E))
    return {"h_sage": bf(h * t),
            "w1b": bf(np.random.standard_normal((E, F)) / np.sqrt(E) / t[:, None]),
            "w2b": bf(np.random.standard_normal((E, F)) / np.sqrt(E) / t[:, None]),
            "gamma": bf(1.0 + 0.2 * np.random.standard_normal(F)),
            "beta": bf(0.3 * np.random.standard_normal(F))}


def reference(h_sage, w1b, w2b, gamma, beta):
    h = f64(h_sage)
    neigh = (h.sum(axis=1, keepdims=True) - h) * 0.5
    out = (mxq(h[:, 0, :], 1, "e4m3") @ mxq(f64(w2b), 0, "e4m3")) + (mxq(neigh[:, 0, :], 1, "e4m3") @ mxq(f64(w1b), 0, "e4m3"))
    mean = out.mean(axis=0)
    var = out.var(axis=0)
    out = (out - mean) / np.sqrt(var + BN_EPS) * f64(gamma) + f64(beta)
    return 1.0 / (1.0 + np.exp(-out))

@@ -1,0 +1,228 @@
+from contextlib import ExitStack
+
+import concourse.mybir as mybir
+from concourse.masks import make_identity
+
+F32 = mybir.dt.float32
+BF16 = mybir.dt.bfloat16
+U32 = mybir.dt.uint32
+U8 = mybir.dt.uint8
+FP8X4 = mybir.dt.float8_e4m3fn_x4
+ACT = mybir.ActivationFunctionType
+ALU = mybir.AluOpType
+
+P = 128
+PACK = 4
+K_PASS = P * PACK
+ITEMS, HOPS, FEATS, COLS = 1024, 3, 1024, 1024
+BN_EPS = 1e-5
+
+PASSES = 2 * FEATS // K_PASS
+BANK = 512
+ITEM_TILES = ITEMS // P
+ITEM_HALVES = ITEMS // BANK
+TILES_PER_HALF = BANK // P
+COL_TILES = COLS // P
+PSUM_BANKS = 8
+FIRST_ROUND = PSUM_BANKS // ITEM_HALVES
+AHEAD = 2
+
+FLOPS = 2 * ITEMS * COLS * 2 * FEATS
+
+
+def tile_dogtaitujuanji_pb_kernel(tc, h_sage, w1b, w2b, gamma, beta, out):
+    nc = tc.nc
+    with ExitStack() as ctx:
+        consts = ctx.enter_context(tc.tile_pool(name="consts", bufs=1))
+        keep = ctx.enter_context(tc.tile_pool(name="keep", bufs=1))
+        h_pool = ctx.enter_context(tc.tile_pool(name="h", bufs=ITEM_TILES))
+        mean_pool = ctx.enter_context(tc.tile_pool(name="mean", bufs=3))
+        item_pool = ctx.enter_context(tc.tile_pool(name="item", bufs=3))
+        raw_pool = ctx.enter_context(tc.tile_pool(name="raw", bufs=PASSES))
+        weight_pool = ctx.enter_context(tc.tile_pool(name="weight", bufs=2))
+        small = ctx.enter_context(tc.tile_pool(name="small", bufs=4))
+        sig_pool = ctx.enter_context(tc.tile_pool(name="sig", bufs=AHEAD + 2))
+        out_pool = ctx.enter_context(tc.tile_pool(name="outp", bufs=3))
+        psum = ctx.enter_context(tc.psum_pool(name="psum", bufs=PSUM_BANKS))
+
+        h_tiles = []
+        for nt in range(ITEM_TILES):
+            h_t = h_pool.tile([P, HOPS, FEATS], BF16)
+            nc.sync.dma_start(out=h_t[:], in_=h_sage[nt * P : (nt + 1) * P, :, :])
+            h_tiles.append(h_t)
+        raw_tiles = []
+        for ps in range(PASSES):
+            w = w2b if ps < PASSES // 2 else w1b
+            g = ps % 2
+            raw = raw_pool.tile([P, PACK, COLS], BF16)
+            nc.sync.dma_start(
+                out=raw[:].rearrange("p (u e) c -> p u (e c)", u=2),
+                in_=w[g * K_PASS : (g + 1) * K_PASS, :].rearrange("(u p e) c -> p u (e c)", u=2, e=2),
+            )
+            raw_tiles.append(raw)
+
+        ident_f32 = consts.tile([P, P], F32)
+        make_identity(nc, ident_f32[:])
+        ident_bf16 = consts.tile([P, P], BF16)
+        make_identity(nc, ident_bf16[:])
+        neg_half = consts.tile([P, 1], F32)
+        nc.gpsimd.memset(neg_half[:], -0.5)
+        warm_in = consts.tile([P, 1], F32)
+        warm_out = consts.tile([P, 1], F32)
+        nc.vector.memset(warm_in[:], 0.0)
+        nc.scalar.activation(out=warm_out[:], in_=warm_in[:], func=ACT.Sigmoid)
+        gb_rows = consts.tile([P, P], BF16)
+        nc.vector.memset(gb_rows[:], 0.0)
+        nc.scalar.dma_start(out=gb_rows[0:COL_TILES, :], in_=gamma.rearrange("(t c) -> t c", c=P))
+        nc.scalar.dma_start(out=gb_rows[COL_TILES : 2 * COL_TILES, :], in_=beta.rearrange("(t c) -> t c", c=P))
+
+        act_codes = keep.tile([P, ITEM_HALVES, PASSES, BANK], U32, align_bytes=64)
+        act_scales = keep.tile([P, ITEM_HALVES, PASSES, BANK], U8, align_bytes=64)
+        w_codes = keep.tile([P, PASSES, COLS], U32, align_bytes=64)
+        w_scales = keep.tile([P, PASSES, COLS], U8, align_bytes=64)
+
+        def quantise_items(nt, grouped):
+            half, first = divmod(nt * P, BANK)
+            for ps in range(PASSES):
+                nc.vector.quantize_mx(
+                    out=act_codes[:, half, ps, first : first + P].bitcast(FP8X4),
+                    scales=act_scales[:, half, ps, first : first + P],
+                    in_=grouped[:, ps, :, :].rearrange("p n t -> p (n t)"),
+                )
+
+        grouped_tiles = []
+        for nt in range(ITEM_TILES):
+            h_t = h_tiles[nt]
+            hop_sum = mean_pool.tile([P, FEATS], BF16)
+            nc.vector.tensor_tensor(out=hop_sum[:], in0=h_t[:, 1, :], in1=h_t[:, 2, :], op=ALU.add)
+            neigh = mean_pool.tile([P, FEATS], BF16)
+            nc.vector.tensor_scalar_mul(out=neigh[:], in0=hop_sum[:], scalar1=0.5)
+
+            self_words = h_t[:, 0, :].bitcast(F32)
+            neigh_words = neigh[:].bitcast(F32)
+            self_ps = psum.tile([P, 2, 2, P], F32, tag="bank")
+            neigh_ps = psum.tile([P, 2, 2, P], F32, tag="bank")
+            for words, turned in ((self_words, self_ps), (neigh_words, neigh_ps)):
+                for g in range(2):
+                    for u in range(2):
+                        first = (2 * g + u) * P
+                        nc.tensor.transpose(turned[:, g, u, :], words[:, first : first + P], ident_f32[:])
+
+            grouped = item_pool.tile([P, PASSES, P, PACK], BF16, align_bytes=64)
+            grouped_words = grouped[:].bitcast(F32)
+            nc.scalar.copy(out=grouped_words[:, 0:2, :, :], in_=self_ps[:].rearrange("p g u n -> p g n u"))
+            nc.scalar.copy(out=grouped_words[:, 2:4, :, :], in_=neigh_ps[:].rearrange("p g u n -> p g n u"))
+            grouped_tiles.append(grouped)
+
+            if nt > 0:
+                quantise_items(nt - 1, grouped_tiles[nt - 1])
+        quantise_items(ITEM_TILES - 1, grouped_tiles[ITEM_TILES - 1])
+
+        gb_ps = psum.tile([P, P], BF16, tag="bank")
+        nc.tensor.transpose(gb_ps[:], gb_rows[:], ident_bf16[:])
+        gb = consts.tile([P, 2 * COL_TILES], F32)
+        nc.vector.tensor_copy(out=gb[:], in_=gb_ps[:, 0 : 2 * COL_TILES])
+
+        def regroup(copy, raw, cols, grouped_w):
+            copy(
+                out=grouped_w[:].rearrange("p (c i) t -> p c t i", i=4),
+                in_=raw[:, :, cols].rearrange("p t (c i) -> p c t i", i=4),
+            )
+
+        def quantise_weights(ps, cols, grouped_w):
+            nc.vector.quantize_mx(
+                out=w_codes[:, ps, cols].bitcast(FP8X4),
+                scales=w_scales[:, ps, cols],
+                in_=grouped_w[:].rearrange("p c t -> p (c t)"),
+            )
+
+        def multiply(acc, ct, half, ps):
+            cols = slice(ct * P, (ct + 1) * P)
+            nc.tensor.matmul_mx(
+                out=acc[:],
+                lhsT=w_codes[:, ps, cols].bitcast(FP8X4),
+                lhsT_scale=w_scales[:, ps, cols],
+                rhs=act_codes[:, half, ps, :].bitcast(FP8X4),
+                rhs_scale=act_scales[:, half, ps, :],
+                start=(ps == 0),
+                stop=(ps == PASSES - 1),
+            )
+
+        first_cols = slice(0, FIRST_ROUND * P)
+        later_cols = slice(FIRST_ROUND * P, COLS)
+        acc = {}
+        for ct in range(FIRST_ROUND):
+            for half in range(ITEM_HALVES):
+                acc[(ct, half)] = psum.tile([P, BANK], F32, tag="bank", name="acc")
+        later_tiles = []
+        for ps in range(PASSES):
+            first_w = weight_pool.tile([P, FIRST_ROUND * P, PACK], BF16, align_bytes=64)
+            regroup(nc.vector.tensor_copy, raw_tiles[ps], first_cols, first_w)
+            later_w = weight_pool.tile([P, COLS - FIRST_ROUND * P, PACK], BF16, align_bytes=64)
+            regroup(nc.scalar.copy, raw_tiles[ps], later_cols, later_w)
+            later_tiles.append(later_w)
+            if ps > 0:
+                quantise_weights(ps - 1, later_cols, later_tiles[ps - 1])
+            quantise_weights(ps, first_cols, first_w)
+            for ct in range(FIRST_ROUND):
+                for half in range(ITEM_HALVES):
+                    multiply(acc[(ct, half)], ct, half, ps)
+        quantise_weights(PASSES - 1, later_cols, later_tiles[PASSES - 1])
+
+        sig = {}
+
+        def normalise(ct):
+            stats = small.tile([P, ITEM_HALVES, 6], F32)
+            for half in range(ITEM_HALVES):
+                nc.vector.bn_stats(out=stats[:, half, :], in_=acc[(ct, half)][:])
+            mean_var = small.tile([P, 2], F32)
+            nc.vector.bn_aggr(out=mean_var[:], in_=stats[:].rearrange("p h s -> p (h s)"))
+            var_eps = small.tile([P, 1], F32)
+            nc.vector.tensor_scalar_add(out=var_eps[:], in0=mean_var[:, 1:2], scalar1=BN_EPS)
+            rstd = small.tile([P, 1], F32)
+            nc.gpsimd.tensor_tensor(out=rstd[:], in0=var_eps[:], in1=neg_half[:], op=ALU.pow)
+            scale = small.tile([P, 1], F32)
+            nc.gpsimd.tensor_tensor(out=scale[:], in0=rstd[:], in1=gb[:, ct : ct + 1], op=ALU.mult)
+            mean_scaled = small.tile([P, 1], F32)
+            nc.gpsimd.tensor_tensor(out=mean_scaled[:], in0=mean_var[:, 0:1], in1=scale[:], op=ALU.mult)
+            shift = small.tile([P, 1], F32)
+            nc.gpsimd.tensor_tensor(
+                out=shift[:], in0=gb[:, COL_TILES + ct : COL_TILES + ct + 1], in1=mean_scaled[:], op=ALU.subtract
+            )
+            sig[ct] = sig_pool.tile([P, ITEMS], F32, name="sig")
+            for half in range(ITEM_HALVES):
+                nc.scalar.activation(
+                    out=sig[ct][:, half * BANK : (half + 1) * BANK],
+                    in_=acc[(ct, half)][:],
+                    func=ACT.Sigmoid,
+                    bias=shift[:],
+                    scale=scale[:],
+                )
+
+        def multiply_all(ct):
+            for half in range(ITEM_HALVES):
+                acc[(ct, half)] = psum.tile([P, BANK], F32, tag="bank", name="acc")
+                for ps in range(PASSES):
+                    multiply(acc[(ct, half)], ct, half, ps)
+
+        out_by_tile = out.rearrange("(t p) c -> p t c", p=P)
+
+        def transpose_back(ct):
+            out_ct = out_pool.tile([P, ITEM_TILES, P], F32)
+            for half in range(ITEM_HALVES):
+                back = psum.tile([P, TILES_PER_HALF, P], F32, tag="bank")
+                for i in range(TILES_PER_HALF):
+                    first = half * BANK + i * P
+                    nc.tensor.transpose(back[:, i, :], sig[ct][:, first : first + P], ident_f32[:])
+                copy = nc.vector.tensor_copy if half == 0 else nc.scalar.copy
+                copy(out=out_ct[:, half * TILES_PER_HALF : (half + 1) * TILES_PER_HALF, :], in_=back[:])
+            nc.sync.dma_start(out=out_by_tile[:, :, ct * P : (ct + 1) * P], in_=out_ct[:])
+
+        for ct in range(AHEAD):
+            normalise(ct)
+        for ct in range(COL_TILES):
+            if ct + FIRST_ROUND < COL_TILES:
+                multiply_all(ct + FIRST_ROUND)
+            if ct + AHEAD < COL_TILES:
+                normalise(ct + AHEAD)
+            transpose_back(ct)

@@ -43,6 +43,7 @@ def tile_dogtaitujuanji_pb_kernel(tc, h_sage, w1b, w2b, gamma, beta, out):
         small = ctx.enter_context(tc.tile_pool(name="small", bufs=4))
         sig_pool = ctx.enter_context(tc.tile_pool(name="sig", bufs=AHEAD + 2))
         out_pool = ctx.enter_context(tc.tile_pool(name="outp", bufs=3))
+        park_pool = ctx.enter_context(tc.tile_pool(name="park", bufs=PSUM_BANKS))
         psum = ctx.enter_context(tc.psum_pool(name="psum", bufs=PSUM_BANKS))
 
         h_tiles = []
@@ -175,6 +176,14 @@ def tile_dogtaitujuanji_pb_kernel(tc, h_sage, w1b, w2b, gamma, beta, out):
             stats = small.tile([P, ITEM_HALVES, 6], F32)
             for half in range(ITEM_HALVES):
                 nc.vector.bn_stats(out=stats[:, half, :], in_=acc[(ct, half)][:])
+            source = {}
+            for half in range(ITEM_HALVES):
+                if ct < FIRST_ROUND:
+                    parked = park_pool.tile([P, BANK], F32)
+                    nc.scalar.copy(out=parked[:], in_=acc[(ct, half)][:])
+                    source[half] = parked
+                else:
+                    source[half] = acc[(ct, half)]
             mean_var = small.tile([P, 2], F32)
             nc.vector.bn_aggr(out=mean_var[:], in_=stats[:].rearrange("p h s -> p (h s)"))
             var_eps = small.tile([P, 1], F32)
@@ -193,7 +202,7 @@ def tile_dogtaitujuanji_pb_kernel(tc, h_sage, w1b, w2b, gamma, beta, out):
             for half in range(ITEM_HALVES):
                 nc.scalar.activation(
                     out=sig[ct][:, half * BANK : (half + 1) * BANK],
-                    in_=acc[(ct, half)][:],
+                    in_=source[half][:],
                     func=ACT.Sigmoid,
                     bias=shift[:],
                     scale=scale[:],

from contextlib import ExitStack

import concourse.mybir as mybir
from concourse.masks import make_identity

F32 = mybir.dt.float32
BF16 = mybir.dt.bfloat16
U32 = mybir.dt.uint32
U8 = mybir.dt.uint8
FP8X4 = mybir.dt.float8_e4m3fn_x4
ACT = mybir.ActivationFunctionType
ALU = mybir.AluOpType

P = 128
PACK = 4
K_PASS = P * PACK
ITEMS, HOPS, FEATS, COLS = 1024, 3, 1024, 1024
BN_EPS = 1e-5

PASSES = 2 * FEATS // K_PASS
BANK = 512
ITEM_TILES = ITEMS // P
ITEM_HALVES = ITEMS // BANK
TILES_PER_HALF = BANK // P
COL_TILES = COLS // P
PSUM_BANKS = 8
FIRST_ROUND = PSUM_BANKS // ITEM_HALVES
AHEAD = 2

FLOPS = 2 * ITEMS * COLS * 2 * FEATS


def tile_dogtaitujuanji_pb_kernel(tc, h_sage, w1b, w2b, gamma, beta, out):
    nc = tc.nc
    with ExitStack() as ctx:
        consts = ctx.enter_context(tc.tile_pool(name="consts", bufs=1))
        keep = ctx.enter_context(tc.tile_pool(name="keep", bufs=1))
        h_pool = ctx.enter_context(tc.tile_pool(name="h", bufs=ITEM_TILES))
        mean_pool = ctx.enter_context(tc.tile_pool(name="mean", bufs=3))
        item_pool = ctx.enter_context(tc.tile_pool(name="item", bufs=3))
        raw_pool = ctx.enter_context(tc.tile_pool(name="raw", bufs=PASSES))
        weight_pool = ctx.enter_context(tc.tile_pool(name="weight", bufs=2))
        small = ctx.enter_context(tc.tile_pool(name="small", bufs=4))
        sig_pool = ctx.enter_context(tc.tile_pool(name="sig", bufs=AHEAD + 2))
        out_pool = ctx.enter_context(tc.tile_pool(name="outp", bufs=3))
        park_pool = ctx.enter_context(tc.tile_pool(name="park", bufs=PSUM_BANKS))
        psum = ctx.enter_context(tc.psum_pool(name="psum", bufs=PSUM_BANKS))

        h_tiles = []
        for nt in range(ITEM_TILES):
            h_t = h_pool.tile([P, HOPS, FEATS], BF16)
            nc.sync.dma_start(out=h_t[:], in_=h_sage[nt * P : (nt + 1) * P, :, :])
            h_tiles.append(h_t)
        raw_tiles = []
        for ps in range(PASSES):
            w = w2b if ps < PASSES // 2 else w1b
            g = ps % 2
            raw = raw_pool.tile([P, PACK, COLS], BF16)
            nc.sync.dma_start(
                out=raw[:].rearrange("p (u e) c -> p u (e c)", u=2),
                in_=w[g * K_PASS : (g + 1) * K_PASS, :].rearrange("(u p e) c -> p u (e c)", u=2, e=2),
            )
            raw_tiles.append(raw)

        ident_f32 = consts.tile([P, P], F32)
        make_identity(nc, ident_f32[:])
        ident_bf16 = consts.tile([P, P], BF16)
        make_identity(nc, ident_bf16[:])
        neg_half = consts.tile([P, 1], F32)
        nc.gpsimd.memset(neg_half[:], -0.5)
        warm_in = consts.tile([P, 1], F32)
        warm_out = consts.tile([P, 1], F32)
        nc.vector.memset(warm_in[:], 0.0)
        nc.scalar.activation(out=warm_out[:], in_=warm_in[:], func=ACT.Sigmoid)
        gb_rows = consts.tile([P, P], BF16)
        nc.vector.memset(gb_rows[:], 0.0)
        nc.scalar.dma_start(out=gb_rows[0:COL_TILES, :], in_=gamma.rearrange("(t c) -> t c", c=P))
        nc.scalar.dma_start(out=gb_rows[COL_TILES : 2 * COL_TILES, :], in_=beta.rearrange("(t c) -> t c", c=P))

        act_codes = keep.tile([P, ITEM_HALVES, PASSES, BANK], U32, align_bytes=64)
        act_scales = keep.tile([P, ITEM_HALVES, PASSES, BANK], U8, align_bytes=64)
        w_codes = keep.tile([P, PASSES, COLS], U32, align_bytes=64)
        w_scales = keep.tile([P, PASSES, COLS], U8, align_bytes=64)

        def quantise_items(nt, grouped):
            half, first = divmod(nt * P, BANK)
            for ps in range(PASSES):
                nc.vector.quantize_mx(
                    out=act_codes[:, half, ps, first : first + P].bitcast(FP8X4),
                    scales=act_scales[:, half, ps, first : first + P],
                    in_=grouped[:, ps, :, :].rearrange("p n t -> p (n t)"),
                )

        grouped_tiles = []
        for nt in range(ITEM_TILES):
            h_t = h_tiles[nt]
            hop_sum = mean_pool.tile([P, FEATS], BF16)
            nc.vector.tensor_tensor(out=hop_sum[:], in0=h_t[:, 1, :], in1=h_t[:, 2, :], op=ALU.add)
            neigh = mean_pool.tile([P, FEATS], BF16)
            nc.vector.tensor_scalar_mul(out=neigh[:], in0=hop_sum[:], scalar1=0.5)

            self_words = h_t[:, 0, :].bitcast(F32)
            neigh_words = neigh[:].bitcast(F32)
            self_ps = psum.tile([P, 2, 2, P], F32, tag="bank")
            neigh_ps = psum.tile([P, 2, 2, P], F32, tag="bank")
            for words, turned in ((self_words, self_ps), (neigh_words, neigh_ps)):
                for g in range(2):
                    for u in range(2):
                        first = (2 * g + u) * P
                        nc.tensor.transpose(turned[:, g, u, :], words[:, first : first + P], ident_f32[:])

            grouped = item_pool.tile([P, PASSES, P, PACK], BF16, align_bytes=64)
            grouped_words = grouped[:].bitcast(F32)
            nc.scalar.copy(out=grouped_words[:, 0:2, :, :], in_=self_ps[:].rearrange("p g u n -> p g n u"))
            nc.scalar.copy(out=grouped_words[:, 2:4, :, :], in_=neigh_ps[:].rearrange("p g u n -> p g n u"))
            grouped_tiles.append(grouped)

            if nt > 0:
                quantise_items(nt - 1, grouped_tiles[nt - 1])
        quantise_items(ITEM_TILES - 1, grouped_tiles[ITEM_TILES - 1])

        gb_ps = psum.tile([P, P], BF16, tag="bank")
        nc.tensor.transpose(gb_ps[:], gb_rows[:], ident_bf16[:])
        gb = consts.tile([P, 2 * COL_TILES], F32)
        nc.vector.tensor_copy(out=gb[:], in_=gb_ps[:, 0 : 2 * COL_TILES])

        def regroup(copy, raw, cols, grouped_w):
            copy(
                out=grouped_w[:].rearrange("p (c i) t -> p c t i", i=4),
                in_=raw[:, :, cols].rearrange("p t (c i) -> p c t i", i=4),
            )

        def quantise_weights(ps, cols, grouped_w):
            nc.vector.quantize_mx(
                out=w_codes[:, ps, cols].bitcast(FP8X4),
                scales=w_scales[:, ps, cols],
                in_=grouped_w[:].rearrange("p c t -> p (c t)"),
            )

        def multiply(acc, ct, half, ps):
            cols = slice(ct * P, (ct + 1) * P)
            nc.tensor.matmul_mx(
                out=acc[:],
                lhsT=w_codes[:, ps, cols].bitcast(FP8X4),
                lhsT_scale=w_scales[:, ps, cols],
                rhs=act_codes[:, half, ps, :].bitcast(FP8X4),
                rhs_scale=act_scales[:, half, ps, :],
                start=(ps == 0),
                stop=(ps == PASSES - 1),
            )

        first_cols = slice(0, FIRST_ROUND * P)
        later_cols = slice(FIRST_ROUND * P, COLS)
        acc = {}
        for ct in range(FIRST_ROUND):
            for half in range(ITEM_HALVES):
                acc[(ct, half)] = psum.tile([P, BANK], F32, tag="bank", name="acc")
        later_tiles = []
        for ps in range(PASSES):
            first_w = weight_pool.tile([P, FIRST_ROUND * P, PACK], BF16, align_bytes=64)
            regroup(nc.vector.tensor_copy, raw_tiles[ps], first_cols, first_w)
            later_w = weight_pool.tile([P, COLS - FIRST_ROUND * P, PACK], BF16, align_bytes=64)
            regroup(nc.scalar.copy, raw_tiles[ps], later_cols, later_w)
            later_tiles.append(later_w)
            if ps > 0:
                quantise_weights(ps - 1, later_cols, later_tiles[ps - 1])
            quantise_weights(ps, first_cols, first_w)
            for ct in range(FIRST_ROUND):
                for half in range(ITEM_HALVES):
                    multiply(acc[(ct, half)], ct, half, ps)
        quantise_weights(PASSES - 1, later_cols, later_tiles[PASSES - 1])

        sig = {}

        def normalise(ct):
            stats = small.tile([P, ITEM_HALVES, 6], F32)
            for half in range(ITEM_HALVES):
                nc.vector.bn_stats(out=stats[:, half, :], in_=acc[(ct, half)][:])
            source = {}
            for half in range(ITEM_HALVES):
                if ct < FIRST_ROUND:
                    parked = park_pool.tile([P, BANK], F32)
                    nc.scalar.copy(out=parked[:], in_=acc[(ct, half)][:])
                    source[half] = parked
                else:
                    source[half] = acc[(ct, half)]
            mean_var = small.tile([P, 2], F32)
            nc.vector.bn_aggr(out=mean_var[:], in_=stats[:].rearrange("p h s -> p (h s)"))
            var_eps = small.tile([P, 1], F32)
            nc.vector.tensor_scalar_add(out=var_eps[:], in0=mean_var[:, 1:2], scalar1=BN_EPS)
            rstd = small.tile([P, 1], F32)
            nc.gpsimd.tensor_tensor(out=rstd[:], in0=var_eps[:], in1=neg_half[:], op=ALU.pow)
            scale = small.tile([P, 1], F32)
            nc.gpsimd.tensor_tensor(out=scale[:], in0=rstd[:], in1=gb[:, ct : ct + 1], op=ALU.mult)
            mean_scaled = small.tile([P, 1], F32)
            nc.gpsimd.tensor_tensor(out=mean_scaled[:], in0=mean_var[:, 0:1], in1=scale[:], op=ALU.mult)
            shift = small.tile([P, 1], F32)
            nc.gpsimd.tensor_tensor(
                out=shift[:], in0=gb[:, COL_TILES + ct : COL_TILES + ct + 1], in1=mean_scaled[:], op=ALU.subtract
            )
            sig[ct] = sig_pool.tile([P, ITEMS], F32, name="sig")
            for half in range(ITEM_HALVES):
                nc.scalar.activation(
                    out=sig[ct][:, half * BANK : (half + 1) * BANK],
                    in_=source[half][:],
                    func=ACT.Sigmoid,
                    bias=shift[:],
                    scale=scale[:],
                )

        def multiply_all(ct):
            for half in range(ITEM_HALVES):
                acc[(ct, half)] = psum.tile([P, BANK], F32, tag="bank", name="acc")
                for ps in range(PASSES):
                    multiply(acc[(ct, half)], ct, half, ps)

        out_by_tile = out.rearrange("(t p) c -> p t c", p=P)

        def transpose_back(ct):
            out_ct = out_pool.tile([P, ITEM_TILES, P], F32)
            for half in range(ITEM_HALVES):
                back = psum.tile([P, TILES_PER_HALF, P], F32, tag="bank")
                for i in range(TILES_PER_HALF):
                    first = half * BANK + i * P
                    nc.tensor.transpose(back[:, i, :], sig[ct][:, first : first + P], ident_f32[:])
                copy = nc.vector.tensor_copy if half == 0 else nc.scalar.copy
                copy(out=out_ct[:, half * TILES_PER_HALF : (half + 1) * TILES_PER_HALF, :], in_=back[:])
            nc.sync.dma_start(out=out_by_tile[:, :, ct * P : (ct + 1) * P], in_=out_ct[:])

        for ct in range(AHEAD):
            normalise(ct)
        for ct in range(COL_TILES):
            if ct + FIRST_ROUND < COL_TILES:
                multiply_all(ct + FIRST_ROUND)
            if ct + AHEAD < COL_TILES:
                normalise(ct + AHEAD)
            transpose_back(ct)
